import numpy as np
import ml_dtypes


def mxq(x, axis, fmt="e4m3"):
    dtype, down = {"e4m3": (ml_dtypes.float8_e4m3fn, 7), "e5m2": (ml_dtypes.float8_e5m2, 14)}[fmt]
    v = np.moveaxis(np.asarray(x, np.float32).astype(ml_dtypes.bfloat16).astype(np.float64), axis, -1)
    blocks = v.reshape(v.shape[:-1] + (-1, 32))
    amax = np.abs(blocks).max(-1, keepdims=True)
    byte = np.maximum(np.where(amax > 0, np.frexp(amax)[1] - 1 + 127, 0) - down, 1)
    scale = np.exp2(byte - 127.0)
    codes = (blocks / scale).astype(np.float32).astype(dtype).astype(np.float64)
    return np.moveaxis((codes * scale).reshape(v.shape), -1, axis)


WIDE = False


def mx_kscale(k):
    if not WIDE:
        return np.ones(k)
    levels = np.array([10, -10, 5, -5, 0])
    a = np.random.permutation(np.resize(levels, k // 512 * 4)).reshape(k // 512, 4)
    idx = np.arange(k)
    return np.exp2(a[idx // 512, idx % 128 // 32])


BF16 = ml_dtypes.bfloat16


def bf(x):
    return np.asarray(x, np.float32).astype(BF16)


def f64(x):
    return np.asarray(x).astype(np.float64)


B, T, C, HS, DW, DA, DV, DG = 4, 128, 2048, 64, 512, 128, 128, 224


def softplus(z):
    return np.logaddexp(0.0, z)


def setup_inputs():
    s = mx_kscale(C)
    return {
        "x": bf(np.random.standard_normal((B, T, C)) * s),
        "x_w": bf(np.random.uniform(0.0, 1.0, C)),
        "w0": bf(np.random.standard_normal(C)),
        "w1": bf(np.random.standard_normal((C, DW)) / np.sqrt(C) / s[:, None]),
        "w2": bf(np.random.standard_normal((DW, C)) / np.sqrt(DW)),
    }


def reference(x, x_w, w0, w1, w2):
    x = f64(x)
    xprev = np.concatenate([np.zeros_like(x[:, :1]), x[:, :-1]], axis=1)
    xx = xprev - x
    xw = x + xx * f64(x_w)
    h = np.tanh(mxq(xw, 2, "e4m3") @ mxq(f64(w1), 0, "e4m3"))
    z = f64(w0) + (mxq(h, 2, "e4m3") @ mxq(f64(w2), 0, "e4m3"))
    return -softplus(-z) - 0.5

@@ -1,0 +1,207 @@
+from contextlib import ExitStack
+
+from concourse import mybir
+from concourse.masks import make_identity
+
+BF16 = mybir.dt.bfloat16
+F32 = mybir.dt.float32
+U32 = mybir.dt.uint32
+U8 = mybir.dt.uint8
+FP8X4 = mybir.dt.float8_e4m3fn_x4
+ALU = mybir.AluOpType
+ACT = mybir.ActivationFunctionType
+
+P = 128
+PACK = 4
+K_PASS = P * PACK
+BATCH = 4
+T = 128
+TOKENS = BATCH * T
+C = 2048
+DW = 512
+C_PASSES = C // K_PASS
+N_BANK = 512
+C_BANKS = C // N_BANK
+HALF = C // 2
+TINY = 2.0 ** -60
+
+FLOPS = 2 * TOKENS * C * DW * 2
+
+
+def regroup(engine_copy, grouped, planes):
+    engine_copy(
+        out=grouped.rearrange("p (c i) j -> p c j i", i=4),
+        in_=planes.rearrange("p j (c i) -> p c j i", i=4),
+    )
+
+
+def quantise(nc, grouped, codes, scales):
+    nc.vector.quantize_mx(
+        out=codes.bitcast(FP8X4),
+        scales=scales,
+        in_=grouped.rearrange("p w j -> p (w j)"),
+    )
+
+
+def tile_full_tmix_params_pc_kernel(tc, x, x_w, w0, w1, w2, out):
+    nc = tc.nc
+    with ExitStack() as stack:
+        const = stack.enter_context(tc.tile_pool(name="const", bufs=1))
+        keep = stack.enter_context(tc.tile_pool(name="keep", bufs=1))
+        work = stack.enter_context(tc.tile_pool(name="work", bufs=2))
+        psum = stack.enter_context(tc.psum_pool(name="psum", bufs=8))
+
+        ident = const.tile([P, P], BF16, name="ident")
+        make_identity(nc, ident[:])
+        half = const.tile([P, 1], F32, name="half")
+        nc.vector.memset(half[:], 0.5)
+        tiny = const.tile([P, 1], F32, name="tiny")
+        nc.vector.memset(tiny[:], TINY)
+        warm = const.tile([P, 1], F32, name="warm")
+        nc.scalar.activation(out=warm[:], in_=half[:], func=ACT.Sigmoid)
+
+        xw_rows = const.tile([P, P], BF16, name="xw_rows")
+        nc.vector.memset(xw_rows[:], 0.0)
+        nc.sync.dma_start(
+            out=xw_rows[0 : C // P, :], in_=x_w.rearrange("(r c) -> r c", c=P)
+        )
+        x_by_token = x.rearrange("b t c -> t b c")
+        x_sb = []
+        w1_sb = []
+        for g in range(C_PASSES):
+            k_rows = slice(g * K_PASS, (g + 1) * K_PASS)
+            x_g = keep.tile([P, BATCH, K_PASS], BF16, name="x_sb%d" % g)
+            nc.sync.dma_start(out=x_g[:], in_=x_by_token[:, :, k_rows])
+            x_sb.append(x_g)
+            w1_g = keep.tile([P, PACK, DW], BF16, name="w1_sb%d" % g)
+            nc.sync.dma_start(
+                out=w1_g[:], in_=w1[k_rows, :].rearrange("(j p) n -> p j n", p=P)
+            )
+            w1_sb.append(w1_g)
+        w2_by_k = w2.rearrange("(j p) n -> p j n", p=P)
+        w2_sb = []
+        for c in range(C_BANKS):
+            w2_c = keep.tile([P, PACK, N_BANK], BF16, name="w2_sb%d" % c)
+            nc.sync.dma_start(out=w2_c[:], in_=w2_by_k[:, :, c * N_BANK : (c + 1) * N_BANK])
+            w2_sb.append(w2_c)
+        w0_bc = const.tile([P, C], BF16, name="w0_bc")
+        nc.sync.dma_start(out=w0_bc[:], in_=w0.partition_broadcast(P))
+
+        mix_ps = psum.tile([P, P], BF16, name="mix_ps", tag="bank")
+        nc.tensor.transpose(mix_ps[:], xw_rows[:], ident[:])
+        mix = const.tile([P, C // P], F32, name="mix")
+        nc.vector.tensor_copy(out=mix[:], in_=mix_ps[:, 0 : C // P])
+        one_minus_mix = const.tile([P, C // P], F32, name="one_minus_mix")
+        nc.vector.tensor_scalar(
+            out=one_minus_mix[:], in0=mix_ps[:, 0 : C // P],
+            scalar1=-1.0, scalar2=1.0, op0=ALU.mult, op1=ALU.add,
+        )
+
+        prev = []
+        for i in range(PACK):
+            prev_i = keep.tile([P, BATCH, T + 1], F32, name="prev%d" % i)
+            nc.vector.memset(prev_i[:], 0.0)
+            prev.append(prev_i)
+
+        x_codes = keep.tile([P, C_PASSES, TOKENS], U32, name="x_codes", align_bytes=64)
+        x_scales = keep.tile([P, C_PASSES, TOKENS], U8, name="x_scales", align_bytes=64)
+        w1_codes = keep.tile([P, C_PASSES, DW], U32, name="w1_codes", align_bytes=64)
+        w1_scales = keep.tile([P, C_PASSES, DW], U8, name="w1_scales", align_bytes=64)
+        w2_codes = keep.tile([P, C_BANKS, N_BANK], U32, name="w2_codes", align_bytes=64)
+        w2_scales = keep.tile([P, C_BANKS, N_BANK], U8, name="w2_scales", align_bytes=64)
+        h_codes = keep.tile([P, BATCH, T], U32, name="h_codes", align_bytes=64)
+        h_scales = keep.tile([P, BATCH, T], U8, name="h_scales", align_bytes=64)
+
+        for g in range(C_PASSES):
+            xw_planes = work.tile([P, PACK, BATCH, T], BF16, name="xw_planes")
+            for j in range(PACK):
+                chunk = g * PACK + j
+                xT = psum.tile([P, BATCH, T], BF16, name="xT", tag="bank")
+                for b in range(BATCH):
+                    nc.tensor.transpose(xT[:, b, :], x_sb[g][:, b, j * P : (j + 1) * P], ident[:])
+                nc.scalar.activation(
+                    out=prev[j][:, :, 1 : T + 1], in_=xT[:], func=ACT.Copy,
+                    scale=mix[:, chunk : chunk + 1],
+                )
+                nc.vector.scalar_tensor_tensor(
+                    out=xw_planes[:, j, :, :], in0=xT[:],
+                    scalar=one_minus_mix[:, chunk : chunk + 1],
+                    in1=prev[j][:, :, 0:T], op0=ALU.mult, op1=ALU.add,
+                )
+            w1_grouped = work.tile([P, DW, PACK], BF16, name="w1_grouped", align_bytes=64)
+            regroup(nc.scalar.copy, w1_grouped[:], w1_sb[g][:])
+            xw_grouped = work.tile([P, TOKENS, PACK], BF16, name="xw_grouped", align_bytes=64)
+            regroup(
+                nc.vector.tensor_copy, xw_grouped[:],
+                xw_planes[:].rearrange("p j b t -> p j (b t)"),
+            )
+            quantise(nc, w1_grouped[:], w1_codes[:, g, :], w1_scales[:, g, :])
+            quantise(nc, xw_grouped[:], x_codes[:, g, :], x_scales[:, g, :])
+
+        for c in range(C_BANKS):
+            w2_grouped = work.tile([P, N_BANK, PACK], BF16, name="w2_grouped", bufs=4, align_bytes=64)
+            if c < C_BANKS // 2:
+                regroup(nc.scalar.copy, w2_grouped[:], w2_sb[c][:])
+            else:
+                regroup(nc.vector.tensor_copy, w2_grouped[:], w2_sb[c][:])
+            quantise(nc, w2_grouped[:], w2_codes[:, c, :], w2_scales[:, c, :])
+
+        z_all = []
+        s_all = []
+        for b in range(BATCH):
+            tok = slice(b * T, (b + 1) * T)
+            hT = psum.tile([P, PACK, T], F32, name="hT", tag="bank")
+            for m in range(PACK):
+                units = slice(m * P, (m + 1) * P)
+                for g in range(C_PASSES):
+                    nc.tensor.matmul_mx(
+                        out=hT[:, m, :],
+                        lhsT=w1_codes[:, g, units].bitcast(FP8X4),
+                        lhsT_scale=w1_scales[:, g, units],
+                        rhs=x_codes[:, g, tok].bitcast(FP8X4),
+                        rhs_scale=x_scales[:, g, tok],
+                        start=(g == 0),
+                        stop=(g == C_PASSES - 1),
+                    )
+            h_grouped = work.tile([P, T, PACK], BF16, name="h_grouped", align_bytes=64)
+            nc.scalar.activation(
+                out=h_grouped[:], in_=hT[:].rearrange("p m t -> p t m"), func=ACT.Tanh
+            )
+            quantise(nc, h_grouped[:], h_codes[:, b, :], h_scales[:, b, :])
+
+            z = keep.tile([P, C], F32, name="z%d" % b)
+            s = keep.tile([P, C], F32, name="s%d" % b)
+            for c in range(C_BANKS):
+                cols = slice(c * N_BANK, (c + 1) * N_BANK)
+                z_ps = psum.tile([P, N_BANK], F32, name="z_ps", tag="bank")
+                nc.tensor.matmul_mx(
+                    out=z_ps[:],
+                    lhsT=h_codes[:, b, :].bitcast(FP8X4),
+                    lhsT_scale=h_scales[:, b, :],
+                    rhs=w2_codes[:, c, :].bitcast(FP8X4),
+                    rhs_scale=w2_scales[:, c, :],
+                    start=True,
+                    stop=True,
+                )
+                nc.vector.scalar_tensor_tensor(
+                    out=z[:, cols], in0=z_ps[:], scalar=-0.5, in1=w0_bc[:, cols],
+                    op0=ALU.add, op1=ALU.add,
+                )
+            for piece in range(C // HALF):
+                cols = slice(piece * HALF, (piece + 1) * HALF)
+                nc.scalar.activation(
+                    out=s[:, cols], in_=z[:, cols], func=ACT.Sigmoid, bias=half[:]
+                )
+            z_all.append(z)
+            s_all.append(s)
+
+        for b in range(BATCH):
+            for piece in range(C // HALF):
+                cols = slice(piece * HALF, (piece + 1) * HALF)
+                s = s_all[b]
+                nc.scalar.activation(out=s[:, cols], in_=s[:, cols], func=ACT.Ln, bias=tiny[:])
+                nc.vector.scalar_tensor_tensor(
+                    out=s[:, cols], in0=s[:, cols], scalar=-0.5, in1=z_all[b][:, cols],
+                    op0=ALU.add, op1=ALU.min,
+                )
+                nc.sync.dma_start(out=out[b, :, cols], in_=s[:, cols])

@@ -50,6 +50,7 @@ def tile_full_tmix_params_pc_kernel(tc, x, x_w, w0, w1, w2, out):
         keep = stack.enter_context(tc.tile_pool(name="keep", bufs=1))
         work = stack.enter_context(tc.tile_pool(name="work", bufs=2))
         psum = stack.enter_context(tc.psum_pool(name="psum", bufs=8))
+        stack.enter_context(tc.manual_schedule())
 
         ident = const.tile([P, P], BF16, name="ident")
         make_identity(nc, ident[:])
@@ -128,26 +129,34 @@ def tile_full_tmix_params_pc_kernel(tc, x, x_w, w0, w1, w2, out):
                     scalar=one_minus_mix[:, chunk : chunk + 1],
                     in1=prev[j][:, :, 0:T], op0=ALU.mult, op1=ALU.add,
                 )
-            w1_grouped = work.tile([P, DW, PACK], BF16, name="w1_grouped", align_bytes=64)
-            regroup(nc.scalar.copy, w1_grouped[:], w1_sb[g][:])
             xw_grouped = work.tile([P, TOKENS, PACK], BF16, name="xw_grouped", align_bytes=64)
             regroup(
                 nc.vector.tensor_copy, xw_grouped[:],
                 xw_planes[:].rearrange("p j b t -> p j (b t)"),
             )
-            quantise(nc, w1_grouped[:], w1_codes[:, g, :], w1_scales[:, g, :])
+            if g > 0:
+                quantise(nc, w1_grouped[:], w1_codes[:, g - 1, :], w1_scales[:, g - 1, :])
             quantise(nc, xw_grouped[:], x_codes[:, g, :], x_scales[:, g, :])
+            w1_grouped = work.tile([P, DW, PACK], BF16, name="w1_grouped", align_bytes=64)
+            regroup(nc.scalar.copy, w1_grouped[:], w1_sb[g][:])
+        quantise(
+            nc, w1_grouped[:], w1_codes[:, C_PASSES - 1, :], w1_scales[:, C_PASSES - 1, :]
+        )
 
+        w2_grouped = []
         for c in range(C_BANKS):
-            w2_grouped = work.tile([P, N_BANK, PACK], BF16, name="w2_grouped", bufs=4, align_bytes=64)
+            w2_grouped_c = work.tile(
+                [P, N_BANK, PACK], BF16, name="w2_grouped%d" % c, bufs=1, align_bytes=64
+            )
             if c < C_BANKS // 2:
-                regroup(nc.scalar.copy, w2_grouped[:], w2_sb[c][:])
+                regroup(nc.vector.tensor_copy, w2_grouped_c[:], w2_sb[c][:])
             else:
-                regroup(nc.vector.tensor_copy, w2_grouped[:], w2_sb[c][:])
-            quantise(nc, w2_grouped[:], w2_codes[:, c, :], w2_scales[:, c, :])
+                regroup(nc.scalar.copy, w2_grouped_c[:], w2_sb[c][:])
+            w2_grouped.append(w2_grouped_c)
+        for c in range(C_BANKS):
+            quantise(nc, w2_grouped[c][:], w2_codes[:, c, :], w2_scales[:, c, :])
 
-        z_all = []
-        s_all = []
+        h_grouped = []
         for b in range(BATCH):
             tok = slice(b * T, (b + 1) * T)
             hT = psum.tile([P, PACK, T], F32, name="hT", tag="bank")
@@ -163,12 +172,18 @@ def tile_full_tmix_params_pc_kernel(tc, x, x_w, w0, w1, w2, out):
                         start=(g == 0),
                         stop=(g == C_PASSES - 1),
                     )
-            h_grouped = work.tile([P, T, PACK], BF16, name="h_grouped", align_bytes=64)
-            nc.scalar.activation(
-                out=h_grouped[:], in_=hT[:].rearrange("p m t -> p t m"), func=ACT.Tanh
+            h_grouped_b = work.tile(
+                [P, T, PACK], BF16, name="h_grouped%d" % b, bufs=1, align_bytes=64
             )
-            quantise(nc, h_grouped[:], h_codes[:, b, :], h_scales[:, b, :])
+            nc.scalar.activation(
+                out=h_grouped_b[:], in_=hT[:].rearrange("p m t -> p t m"), func=ACT.Tanh
+            )
+            h_grouped.append(h_grouped_b)
 
+        z_all = []
+        s_all = []
+        quantise(nc, h_grouped[0][:], h_codes[:, 0, :], h_scales[:, 0, :])
+        for b in range(BATCH):
             z = keep.tile([P, C], F32, name="z%d" % b)
             s = keep.tile([P, C], F32, name="s%d" % b)
             for c in range(C_BANKS):
@@ -187,6 +202,10 @@ def tile_full_tmix_params_pc_kernel(tc, x, x_w, w0, w1, w2, out):
                     out=z[:, cols], in0=z_ps[:], scalar=-0.5, in1=w0_bc[:, cols],
                     op0=ALU.add, op1=ALU.add,
                 )
+                if c == 0 and b + 1 < BATCH:
+                    quantise(
+                        nc, h_grouped[b + 1][:], h_codes[:, b + 1, :], h_scales[:, b + 1, :]
+                    )
             for piece in range(C // HALF):
                 cols = slice(piece * HALF, (piece + 1) * HALF)
                 nc.scalar.activation(

@@ -22,7 +22,7 @@ DW = 512
 C_PASSES = C // K_PASS
 N_BANK = 512
 C_BANKS = C // N_BANK
-HALF = C // 2
+WIDE = 1024
 TINY = 2.0 ** -60
 
 FLOPS = 2 * TOKENS * C * DW * 2
@@ -54,6 +54,8 @@ def tile_full_tmix_params_pc_kernel(tc, x, x_w, w0, w1, w2, out):
 
         ident = const.tile([P, P], BF16, name="ident")
         make_identity(nc, ident[:])
+        xw_rows = const.tile([P, P], BF16, name="xw_rows")
+        nc.vector.memset(xw_rows[:], 0.0)
         half = const.tile([P, 1], F32, name="half")
         nc.vector.memset(half[:], 0.5)
         tiny = const.tile([P, 1], F32, name="tiny")
@@ -61,8 +63,6 @@ def tile_full_tmix_params_pc_kernel(tc, x, x_w, w0, w1, w2, out):
         warm = const.tile([P, 1], F32, name="warm")
         nc.scalar.activation(out=warm[:], in_=half[:], func=ACT.Sigmoid)
 
-        xw_rows = const.tile([P, P], BF16, name="xw_rows")
-        nc.vector.memset(xw_rows[:], 0.0)
         nc.sync.dma_start(
             out=xw_rows[0 : C // P, :], in_=x_w.rearrange("(r c) -> r c", c=P)
         )
@@ -70,13 +70,19 @@ def tile_full_tmix_params_pc_kernel(tc, x, x_w, w0, w1, w2, out):
         x_sb = []
         w1_sb = []
         for g in range(C_PASSES):
-            k_rows = slice(g * K_PASS, (g + 1) * K_PASS)
             x_g = keep.tile([P, BATCH, K_PASS], BF16, name="x_sb%d" % g)
-            nc.sync.dma_start(out=x_g[:], in_=x_by_token[:, :, k_rows])
+            loads = PACK if g == 0 else 1
+            width = K_PASS // loads
+            for i in range(loads):
+                nc.sync.dma_start(
+                    out=x_g[:, :, i * width : (i + 1) * width],
+                    in_=x_by_token[:, :, g * K_PASS + i * width : g * K_PASS + (i + 1) * width],
+                )
             x_sb.append(x_g)
             w1_g = keep.tile([P, PACK, DW], BF16, name="w1_sb%d" % g)
             nc.sync.dma_start(
-                out=w1_g[:], in_=w1[k_rows, :].rearrange("(j p) n -> p j n", p=P)
+                out=w1_g[:],
+                in_=w1[g * K_PASS : (g + 1) * K_PASS, :].rearrange("(j p) n -> p j n", p=P),
             )
             w1_sb.append(w1_g)
         w2_by_k = w2.rearrange("(j p) n -> p j n", p=P)
@@ -88,6 +94,12 @@ def tile_full_tmix_params_pc_kernel(tc, x, x_w, w0, w1, w2, out):
         w0_bc = const.tile([P, C], BF16, name="w0_bc")
         nc.sync.dma_start(out=w0_bc[:], in_=w0.partition_broadcast(P))
 
+        prev = []
+        for j in range(PACK):
+            prev_j = keep.tile([P, BATCH, T + 1], F32, name="prev%d" % j)
+            nc.vector.memset(prev_j[:], 0.0)
+            prev.append(prev_j)
+
         mix_ps = psum.tile([P, P], BF16, name="mix_ps", tag="bank")
         nc.tensor.transpose(mix_ps[:], xw_rows[:], ident[:])
         mix = const.tile([P, C // P], F32, name="mix")
@@ -98,12 +110,6 @@ def tile_full_tmix_params_pc_kernel(tc, x, x_w, w0, w1, w2, out):
             scalar1=-1.0, scalar2=1.0, op0=ALU.mult, op1=ALU.add,
         )
 
-        prev = []
-        for i in range(PACK):
-            prev_i = keep.tile([P, BATCH, T + 1], F32, name="prev%d" % i)
-            nc.vector.memset(prev_i[:], 0.0)
-            prev.append(prev_i)
-
         x_codes = keep.tile([P, C_PASSES, TOKENS], U32, name="x_codes", align_bytes=64)
         x_scales = keep.tile([P, C_PASSES, TOKENS], U8, name="x_scales", align_bytes=64)
         w1_codes = keep.tile([P, C_PASSES, DW], U32, name="w1_codes", align_bytes=64)
@@ -113,6 +119,8 @@ def tile_full_tmix_params_pc_kernel(tc, x, x_w, w0, w1, w2, out):
         h_codes = keep.tile([P, BATCH, T], U32, name="h_codes", align_bytes=64)
         h_scales = keep.tile([P, BATCH, T], U8, name="h_scales", align_bytes=64)
 
+        xw_grouped = []
+        w1_grouped = []
         for g in range(C_PASSES):
             xw_planes = work.tile([P, PACK, BATCH, T], BF16, name="xw_planes")
             for j in range(PACK):
@@ -129,35 +137,26 @@ def tile_full_tmix_params_pc_kernel(tc, x, x_w, w0, w1, w2, out):
                     scalar=one_minus_mix[:, chunk : chunk + 1],
                     in1=prev[j][:, :, 0:T], op0=ALU.mult, op1=ALU.add,
                 )
-            xw_grouped = work.tile([P, TOKENS, PACK], BF16, name="xw_grouped", align_bytes=64)
+                if j == 0 and g > 0:
+                    quantise(nc, xw_grouped[g - 1][:], x_codes[:, g - 1, :], x_scales[:, g - 1, :])
+            if g > 0:
+                quantise(nc, w1_grouped[g - 1][:], w1_codes[:, g - 1, :], w1_scales[:, g - 1, :])
+            xw_grouped.append(
+                work.tile([P, TOKENS, PACK], BF16, name="xw_grouped%d" % g, tag="xw_grouped", align_bytes=64)
+            )
             regroup(
-                nc.vector.tensor_copy, xw_grouped[:],
+                nc.vector.tensor_copy, xw_grouped[g][:],
                 xw_planes[:].rearrange("p j b t -> p j (b t)"),
             )
-            if g > 0:
-                quantise(nc, w1_grouped[:], w1_codes[:, g - 1, :], w1_scales[:, g - 1, :])
-            quantise(nc, xw_grouped[:], x_codes[:, g, :], x_scales[:, g, :])
-            w1_grouped = work.tile([P, DW, PACK], BF16, name="w1_grouped", align_bytes=64)
-            regroup(nc.scalar.copy, w1_grouped[:], w1_sb[g][:])
-        quantise(
-            nc, w1_grouped[:], w1_codes[:, C_PASSES - 1, :], w1_scales[:, C_PASSES - 1, :]
-        )
-
-        w2_grouped = []
-        for c in range(C_BANKS):
-            w2_grouped_c = work.tile(
-                [P, N_BANK, PACK], BF16, name="w2_grouped%d" % c, bufs=1, align_bytes=64
+            w1_grouped.append(
+                work.tile([P, DW, PACK], BF16, name="w1_grouped%d" % g, tag="w1_grouped", align_bytes=64)
             )
-            if c < C_BANKS // 2:
-                regroup(nc.vector.tensor_copy, w2_grouped_c[:], w2_sb[c][:])
-            else:
-                regroup(nc.scalar.copy, w2_grouped_c[:], w2_sb[c][:])
-            w2_grouped.append(w2_grouped_c)
-        for c in range(C_BANKS):
-            quantise(nc, w2_grouped[c][:], w2_codes[:, c, :], w2_scales[:, c, :])
+            regroup(nc.scalar.copy, w1_grouped[g][:], w1_sb[g][:])
+        last = C_PASSES - 1
+        quantise(nc, w1_grouped[last][:], w1_codes[:, last, :], w1_scales[:, last, :])
+        quantise(nc, xw_grouped[last][:], x_codes[:, last, :], x_scales[:, last, :])
 
-        h_grouped = []
-        for b in range(BATCH):
+        def hidden(b):
             tok = slice(b * T, (b + 1) * T)
             hT = psum.tile([P, PACK, T], F32, name="hT", tag="bank")
             for m in range(PACK):
@@ -172,18 +171,37 @@ def tile_full_tmix_params_pc_kernel(tc, x, x_w, w0, w1, w2, out):
                         start=(g == 0),
                         stop=(g == C_PASSES - 1),
                     )
-            h_grouped_b = work.tile(
-                [P, T, PACK], BF16, name="h_grouped%d" % b, bufs=1, align_bytes=64
-            )
             nc.scalar.activation(
-                out=h_grouped_b[:], in_=hT[:].rearrange("p m t -> p t m"), func=ACT.Tanh
+                out=h_grouped[b][:], in_=hT[:].rearrange("p m t -> p t m"), func=ACT.Tanh
             )
-            h_grouped.append(h_grouped_b)
+
+        h_grouped = []
+        for b in range(BATCH):
+            h_grouped.append(
+                work.tile([P, T, PACK], BF16, name="h_grouped%d" % b, bufs=1, align_bytes=64)
+            )
+        w2_grouped = []
+        for c in range(C_BANKS):
+            w2_grouped.append(
+                work.tile([P, N_BANK, PACK], BF16, name="w2_grouped%d" % c, bufs=1, align_bytes=64)
+            )
+        regroup(nc.vector.tensor_copy, w2_grouped[0][:], w2_sb[0][:])
+        regroup(nc.vector.tensor_copy, w2_grouped[1][:], w2_sb[1][:])
+        regroup(nc.scalar.copy, w2_grouped[2][:], w2_sb[2][:])
+        hidden(0)
+        regroup(nc.scalar.copy, w2_grouped[3][:], w2_sb[3][:])
+        hidden(1)
+        quantise(nc, w2_grouped[0][:], w2_codes[:, 0, :], w2_scales[:, 0, :])
+        quantise(nc, w2_grouped[1][:], w2_codes[:, 1, :], w2_scales[:, 1, :])
+        quantise(nc, h_grouped[0][:], h_codes[:, 0, :], h_scales[:, 0, :])
+        quantise(nc, w2_grouped[2][:], w2_codes[:, 2, :], w2_scales[:, 2, :])
+        quantise(nc, w2_grouped[3][:], w2_codes[:, 3, :], w2_scales[:, 3, :])
 
         z_all = []
         s_all = []
-        quantise(nc, h_grouped[0][:], h_codes[:, 0, :], h_scales[:, 0, :])
         for b in range(BATCH):
+            if b + 2 < BATCH:
+                hidden(b + 2)
             z = keep.tile([P, C], F32, name="z%d" % b)
             s = keep.tile([P, C], F32, name="s%d" % b)
             for c in range(C_BANKS):
@@ -202,22 +220,21 @@ def tile_full_tmix_params_pc_kernel(tc, x, x_w, w0, w1, w2, out):
                     out=z[:, cols], in0=z_ps[:], scalar=-0.5, in1=w0_bc[:, cols],
                     op0=ALU.add, op1=ALU.add,
                 )
+                nc.scalar.activation(
+                    out=s[:, cols], in_=z[:, cols], func=ACT.Sigmoid, bias=half[:]
+                )
                 if c == 0 and b + 1 < BATCH:
                     quantise(
                         nc, h_grouped[b + 1][:], h_codes[:, b + 1, :], h_scales[:, b + 1, :]
                     )
-            for piece in range(C // HALF):
-                cols = slice(piece * HALF, (piece + 1) * HALF)
-                nc.scalar.activation(
-                    out=s[:, cols], in_=z[:, cols], func=ACT.Sigmoid, bias=half[:]
-                )
             z_all.append(z)
             s_all.append(s)
 
         for b in range(BATCH):
-            for piece in range(C // HALF):
-                cols = slice(piece * HALF, (piece + 1) * HALF)
-                s = s_all[b]
+            width = WIDE if 0 < b < BATCH - 1 else N_BANK
+            s = s_all[b]
+            for piece in range(C // width):
+                cols = slice(piece * width, (piece + 1) * width)
                 nc.scalar.activation(out=s[:, cols], in_=s[:, cols], func=ACT.Ln, bias=tiny[:])
                 nc.vector.scalar_tensor_tensor(
                     out=s[:, cols], in0=s[:, cols], scalar=-0.5, in1=z_all[b][:, cols],

@@ -49,7 +49,7 @@ def tile_full_tmix_params_pc_kernel(tc, x, x_w, w0, w1, w2, out):
         const = stack.enter_context(tc.tile_pool(name="const", bufs=1))
         keep = stack.enter_context(tc.tile_pool(name="keep", bufs=1))
         work = stack.enter_context(tc.tile_pool(name="work", bufs=2))
-        psum = stack.enter_context(tc.psum_pool(name="psum", bufs=8))
+        psum = stack.enter_context(tc.psum_pool(name="psum", bufs=4))
         stack.enter_context(tc.manual_schedule())
 
         ident = const.tile([P, P], BF16, name="ident")
@@ -60,6 +60,11 @@ def tile_full_tmix_params_pc_kernel(tc, x, x_w, w0, w1, w2, out):
         nc.vector.memset(half[:], 0.5)
         tiny = const.tile([P, 1], F32, name="tiny")
         nc.vector.memset(tiny[:], TINY)
+        diff = const.tile([P, P], BF16, name="diff")
+        nc.vector.tensor_scalar_mul(out=diff[:], in0=ident[:], scalar1=-1.0)
+        nc.vector.tensor_tensor(
+            out=diff[:, 1:P], in0=diff[:, 1:P], in1=ident[:, 0 : P - 1], op=ALU.add
+        )
         warm = const.tile([P, 1], F32, name="warm")
         nc.scalar.activation(out=warm[:], in_=half[:], func=ACT.Sigmoid)
 
@@ -69,7 +74,8 @@ def tile_full_tmix_params_pc_kernel(tc, x, x_w, w0, w1, w2, out):
         x_by_token = x.rearrange("b t c -> t b c")
         x_sb = []
         w1_sb = []
-        for g in range(C_PASSES):
+
+        def load_x(g):
             x_g = keep.tile([P, BATCH, K_PASS], BF16, name="x_sb%d" % g)
             loads = PACK if g == 0 else 1
             width = K_PASS // loads
@@ -79,12 +85,20 @@ def tile_full_tmix_params_pc_kernel(tc, x, x_w, w0, w1, w2, out):
                     in_=x_by_token[:, :, g * K_PASS + i * width : g * K_PASS + (i + 1) * width],
                 )
             x_sb.append(x_g)
+
+        def load_w1(g):
             w1_g = keep.tile([P, PACK, DW], BF16, name="w1_sb%d" % g)
             nc.sync.dma_start(
                 out=w1_g[:],
                 in_=w1[g * K_PASS : (g + 1) * K_PASS, :].rearrange("(j p) n -> p j n", p=P),
             )
             w1_sb.append(w1_g)
+
+        load_x(0)
+        for g in range(1, C_PASSES):
+            load_x(g)
+            load_w1(g - 1)
+        load_w1(C_PASSES - 1)
         w2_by_k = w2.rearrange("(j p) n -> p j n", p=P)
         w2_sb = []
         for c in range(C_BANKS):
@@ -97,10 +111,10 @@ def tile_full_tmix_params_pc_kernel(tc, x, x_w, w0, w1, w2, out):
         prev = []
         for j in range(PACK):
             prev_j = keep.tile([P, BATCH, T + 1], F32, name="prev%d" % j)
-            nc.vector.memset(prev_j[:], 0.0)
+            nc.vector.memset(prev_j[:, :, 0:1], 0.0)
             prev.append(prev_j)
 
-        mix_ps = psum.tile([P, P], BF16, name="mix_ps", tag="bank")
+        mix_ps = psum.tile([P, P], BF16, name="mix_ps", tag="bank_a")
         nc.tensor.transpose(mix_ps[:], xw_rows[:], ident[:])
         mix = const.tile([P, C // P], F32, name="mix")
         nc.vector.tensor_copy(out=mix[:], in_=mix_ps[:, 0 : C // P])
@@ -122,43 +136,86 @@ def tile_full_tmix_params_pc_kernel(tc, x, x_w, w0, w1, w2, out):
         xw_grouped = []
         w1_grouped = []
         for g in range(C_PASSES):
-            xw_planes = work.tile([P, PACK, BATCH, T], BF16, name="xw_planes")
+            xw_grouped.append(
+                work.tile([P, TOKENS, PACK], BF16, name="xw_grouped%d" % g, bufs=1, align_bytes=64)
+            )
+            w1_grouped.append(
+                work.tile([P, DW, PACK], BF16, name="w1_grouped%d" % g, bufs=1, align_bytes=64)
+            )
+        h_grouped = []
+        for b in range(BATCH):
+            h_grouped.append(
+                work.tile([P, T, PACK], BF16, name="h_grouped%d" % b, bufs=1, align_bytes=64)
+            )
+        w2_grouped = []
+        for c in range(C_BANKS):
+            w2_grouped.append(
+                work.tile([P, N_BANK, PACK], BF16, name="w2_grouped%d" % c, bufs=1, align_bytes=64)
+            )
+        xw_planes = work.tile([P, PACK, BATCH, T], BF16, name="xw_planes", bufs=1)
+
+        def first_pass():
             for j in range(PACK):
-                chunk = g * PACK + j
-                xT = psum.tile([P, BATCH, T], BF16, name="xT", tag="bank")
+                xT = psum.tile([P, BATCH, T], BF16, name="xT", tag="bank_b")
                 for b in range(BATCH):
-                    nc.tensor.transpose(xT[:, b, :], x_sb[g][:, b, j * P : (j + 1) * P], ident[:])
+                    nc.tensor.transpose(xT[:, b, :], x_sb[0][:, b, j * P : (j + 1) * P], ident[:])
                 nc.scalar.activation(
                     out=prev[j][:, :, 1 : T + 1], in_=xT[:], func=ACT.Copy,
-                    scale=mix[:, chunk : chunk + 1],
+                    scale=mix[:, j : j + 1],
                 )
                 nc.vector.scalar_tensor_tensor(
                     out=xw_planes[:, j, :, :], in0=xT[:],
-                    scalar=one_minus_mix[:, chunk : chunk + 1],
+                    scalar=one_minus_mix[:, j : j + 1],
                     in1=prev[j][:, :, 0:T], op0=ALU.mult, op1=ALU.add,
                 )
-                if j == 0 and g > 0:
-                    quantise(nc, xw_grouped[g - 1][:], x_codes[:, g - 1, :], x_scales[:, g - 1, :])
-            if g > 0:
-                quantise(nc, w1_grouped[g - 1][:], w1_codes[:, g - 1, :], w1_scales[:, g - 1, :])
-            xw_grouped.append(
-                work.tile([P, TOKENS, PACK], BF16, name="xw_grouped%d" % g, tag="xw_grouped", align_bytes=64)
+
+        halves = {}
+        dms = {}
+
+        def diff_pass(g):
+            halves[g] = []
+            for h in range(2):
+                halves[g].append(
+                    psum.tile([P, PACK, TOKENS // 2], BF16, name="xT_half%d" % h, tag="bank_a")
+                )
+            dms[g] = work.tile([P, PACK, TOKENS], F32, name="dm")
+            for j in range(PACK):
+                chunk = g * PACK + j
+                d_ps = psum.tile([P, BATCH, T], F32, name="d_ps", tag="bank_b")
+                for b in range(BATCH):
+                    block = x_sb[g][:, b, j * P : (j + 1) * P]
+                    t0 = (b % 2) * T
+                    nc.tensor.transpose(halves[g][b // 2][:, j, t0 : t0 + T], block, ident[:])
+                    nc.tensor.matmul(d_ps[:, b, :], lhsT=block, rhs=diff[:], start=True, stop=True)
+                nc.scalar.activation(
+                    out=dms[g][:, j, :], in_=d_ps[:].rearrange("p b t -> p (b t)"), func=ACT.Copy,
+                    scale=mix[:, chunk : chunk + 1],
+                )
+
+        def add_mix(g, h):
+            toks = slice(h * TOKENS // 2, (h + 1) * TOKENS // 2)
+            nc.vector.tensor_tensor(
+                out=xw_grouped[g][:, toks, :].rearrange("p (c i) j -> p c j i", i=4),
+                in0=halves[g][h][:].rearrange("p j (c i) -> p c j i", i=4),
+                in1=dms[g][:, :, toks].rearrange("p j (c i) -> p c j i", i=4),
+                op=ALU.add,
             )
-            regroup(
-                nc.vector.tensor_copy, xw_grouped[g][:],
-                xw_planes[:].rearrange("p j b t -> p j (b t)"),
-            )
-            w1_grouped.append(
-                work.tile([P, DW, PACK], BF16, name="w1_grouped%d" % g, tag="w1_grouped", align_bytes=64)
-            )
-            regroup(nc.scalar.copy, w1_grouped[g][:], w1_sb[g][:])
-        last = C_PASSES - 1
-        quantise(nc, w1_grouped[last][:], w1_codes[:, last, :], w1_scales[:, last, :])
-        quantise(nc, xw_grouped[last][:], x_codes[:, last, :], x_scales[:, last, :])
+
+        def quantise_x(g, toks=slice(0, TOKENS)):
+            quantise(nc, xw_grouped[g][:, toks, :], x_codes[:, g, toks], x_scales[:, g, toks])
+
+        def quantise_w1(g):
+            quantise(nc, w1_grouped[g][:], w1_codes[:, g, :], w1_scales[:, g, :])
+
+        def quantise_w2(c):
+            quantise(nc, w2_grouped[c][:], w2_codes[:, c, :], w2_scales[:, c, :])
+
+        def quantise_h(b):
+            quantise(nc, h_grouped[b][:], h_codes[:, b, :], h_scales[:, b, :])
 
         def hidden(b):
             tok = slice(b * T, (b + 1) * T)
-            hT = psum.tile([P, PACK, T], F32, name="hT", tag="bank")
+            hT = psum.tile([P, PACK, T], F32, name="hT", tag="bank_a")
             for m in range(PACK):
                 units = slice(m * P, (m + 1) * P)
                 for g in range(C_PASSES):
@@ -175,27 +232,41 @@ def tile_full_tmix_params_pc_kernel(tc, x, x_w, w0, w1, w2, out):
                 out=h_grouped[b][:], in_=hT[:].rearrange("p m t -> p t m"), func=ACT.Tanh
             )
 
-        h_grouped = []
-        for b in range(BATCH):
-            h_grouped.append(
-                work.tile([P, T, PACK], BF16, name="h_grouped%d" % b, bufs=1, align_bytes=64)
-            )
-        w2_grouped = []
-        for c in range(C_BANKS):
-            w2_grouped.append(
-                work.tile([P, N_BANK, PACK], BF16, name="w2_grouped%d" % c, bufs=1, align_bytes=64)
-            )
-        regroup(nc.vector.tensor_copy, w2_grouped[0][:], w2_sb[0][:])
-        regroup(nc.vector.tensor_copy, w2_grouped[1][:], w2_sb[1][:])
-        regroup(nc.scalar.copy, w2_grouped[2][:], w2_sb[2][:])
+        def on_vector(grouped, planes):
+            regroup(nc.vector.tensor_copy, grouped[:], planes[:])
+
+        def on_scalar(grouped, planes):
+            regroup(nc.scalar.copy, grouped[:], planes[:])
+
+        first_pass()
+        on_vector(w1_grouped[0], w1_sb[0])
+        regroup(
+            nc.vector.tensor_copy, xw_grouped[0][:], xw_planes[:].rearrange("p j b t -> p j (b t)")
+        )
+        diff_pass(1)
+        quantise_w1(0)
+        quantise_x(0)
+        for g in range(1, C_PASSES):
+            on_scalar(w1_grouped[g], w1_sb[g])
+            if g == C_PASSES - 1:
+                on_vector(w2_grouped[0], w2_sb[0])
+                on_vector(w2_grouped[1], w2_sb[1])
+            add_mix(g, 0)
+            add_mix(g, 1)
+            if g < C_PASSES - 1:
+                diff_pass(g + 1)
+            else:
+                quantise_w2(0)
+            quantise_w1(g)
+            quantise_x(g)
+        on_scalar(w2_grouped[2], w2_sb[2])
+        on_scalar(w2_grouped[3], w2_sb[3])
         hidden(0)
-        regroup(nc.scalar.copy, w2_grouped[3][:], w2_sb[3][:])
         hidden(1)
-        quantise(nc, w2_grouped[0][:], w2_codes[:, 0, :], w2_scales[:, 0, :])
-        quantise(nc, w2_grouped[1][:], w2_codes[:, 1, :], w2_scales[:, 1, :])
-        quantise(nc, h_grouped[0][:], h_codes[:, 0, :], h_scales[:, 0, :])
-        quantise(nc, w2_grouped[2][:], w2_codes[:, 2, :], w2_scales[:, 2, :])
-        quantise(nc, w2_grouped[3][:], w2_codes[:, 3, :], w2_scales[:, 3, :])
+        quantise_w2(1)
+        quantise_w2(2)
+        quantise_w2(3)
+        quantise_h(0)
 
         z_all = []
         s_all = []
@@ -206,7 +277,7 @@ def tile_full_tmix_params_pc_kernel(tc, x, x_w, w0, w1, w2, out):
             s = keep.tile([P, C], F32, name="s%d" % b)
             for c in range(C_BANKS):
                 cols = slice(c * N_BANK, (c + 1) * N_BANK)
-                z_ps = psum.tile([P, N_BANK], F32, name="z_ps", tag="bank")
+                z_ps = psum.tile([P, N_BANK], F32, name="z_ps", tag="bank_a" if c % 2 else "bank_b")
                 nc.tensor.matmul_mx(
                     out=z_ps[:],
                     lhsT=h_codes[:, b, :].bitcast(FP8X4),
@@ -224,9 +295,7 @@ def tile_full_tmix_params_pc_kernel(tc, x, x_w, w0, w1, w2, out):
                     out=s[:, cols], in_=z[:, cols], func=ACT.Sigmoid, bias=half[:]
                 )
                 if c == 0 and b + 1 < BATCH:
-                    quantise(
-                        nc, h_grouped[b + 1][:], h_codes[:, b + 1, :], h_scales[:, b + 1, :]
-                    )
+                    quantise_h(b + 1)
             z_all.append(z)
             s_all.append(s)
 

@@ -195,9 +195,9 @@ def tile_full_tmix_params_pc_kernel(tc, x, x_w, w0, w1, w2, out):
         def add_mix(g, h):
             toks = slice(h * TOKENS // 2, (h + 1) * TOKENS // 2)
             nc.vector.tensor_tensor(
-                out=xw_grouped[g][:, toks, :].rearrange("p (c i) j -> p c j i", i=4),
-                in0=halves[g][h][:].rearrange("p j (c i) -> p c j i", i=4),
-                in1=dms[g][:, :, toks].rearrange("p j (c i) -> p c j i", i=4),
+                out=xw_grouped[g][:, toks, :].rearrange("p (c i) j -> p c j i", i=2),
+                in0=halves[g][h][:].rearrange("p j (c i) -> p c j i", i=2),
+                in1=dms[g][:, :, toks].rearrange("p j (c i) -> p c j i", i=2),
                 op=ALU.add,
             )
 
@@ -246,33 +246,33 @@ def tile_full_tmix_params_pc_kernel(tc, x, x_w, w0, w1, w2, out):
         diff_pass(1)
         quantise_w1(0)
         quantise_x(0)
-        for g in range(1, C_PASSES):
+        last = C_PASSES - 1
+        for g in range(1, last):
             on_scalar(w1_grouped[g], w1_sb[g])
-            if g == C_PASSES - 1:
-                on_vector(w2_grouped[0], w2_sb[0])
-                on_vector(w2_grouped[1], w2_sb[1])
             add_mix(g, 0)
             add_mix(g, 1)
-            if g < C_PASSES - 1:
-                diff_pass(g + 1)
-            else:
-                quantise_w2(0)
+            diff_pass(g + 1)
             quantise_w1(g)
             quantise_x(g)
-        on_scalar(w2_grouped[2], w2_sb[2])
-        on_scalar(w2_grouped[3], w2_sb[3])
+        on_vector(w2_grouped[0], w2_sb[0])
+        on_vector(w1_grouped[last], w1_sb[last])
+        for c in range(1, C_BANKS):
+            on_scalar(w2_grouped[c], w2_sb[c])
+        add_mix(last, 0)
+        quantise_w1(last)
+        quantise_x(last, slice(0, TOKENS // 2))
         hidden(0)
         hidden(1)
-        quantise_w2(1)
-        quantise_w2(2)
-        quantise_w2(3)
+        add_mix(last, 1)
+        quantise_w2(0)
+        quantise_x(last, slice(TOKENS // 2, TOKENS))
+        for c in range(1, C_BANKS):
+            quantise_w2(c)
         quantise_h(0)
 
         z_all = []
         s_all = []
         for b in range(BATCH):
-            if b + 2 < BATCH:
-                hidden(b + 2)
             z = keep.tile([P, C], F32, name="z%d" % b)
             s = keep.tile([P, C], F32, name="s%d" % b)
             for c in range(C_BANKS):
@@ -294,7 +294,9 @@ def tile_full_tmix_params_pc_kernel(tc, x, x_w, w0, w1, w2, out):
                 nc.scalar.activation(
                     out=s[:, cols], in_=z[:, cols], func=ACT.Sigmoid, bias=half[:]
                 )
-                if c == 0 and b + 1 < BATCH:
+                if c == 1 and b + 2 < BATCH:
+                    hidden(b + 2)
+                if c == 2 and b + 1 < BATCH:
                     quantise_h(b + 1)
             z_all.append(z)
             s_all.append(s)

@@ -184,13 +184,19 @@ def tile_full_tmix_params_pc_kernel(tc, x, x_w, w0, w1, w2, out):
                 d_ps = psum.tile([P, BATCH, T], F32, name="d_ps", tag="bank_b")
                 for b in range(BATCH):
                     block = x_sb[g][:, b, j * P : (j + 1) * P]
-                    t0 = (b % 2) * T
-                    nc.tensor.transpose(halves[g][b // 2][:, j, t0 : t0 + T], block, ident[:])
                     nc.tensor.matmul(d_ps[:, b, :], lhsT=block, rhs=diff[:], start=True, stop=True)
                 nc.scalar.activation(
                     out=dms[g][:, j, :], in_=d_ps[:].rearrange("p b t -> p (b t)"), func=ACT.Copy,
                     scale=mix[:, chunk : chunk + 1],
                 )
+            for h in range(2):
+                for j in range(PACK):
+                    for b in range(2):
+                        nc.tensor.transpose(
+                            halves[g][h][:, j, b * T : (b + 1) * T],
+                            x_sb[g][:, 2 * h + b, j * P : (j + 1) * P],
+                            ident[:],
+                        )
 
         def add_mix(g, h):
             toks = slice(h * TOKENS // 2, (h + 1) * TOKENS // 2)
@@ -213,24 +219,27 @@ def tile_full_tmix_params_pc_kernel(tc, x, x_w, w0, w1, w2, out):
         def quantise_h(b):
             quantise(nc, h_grouped[b][:], h_codes[:, b, :], h_scales[:, b, :])
 
-        def hidden(b):
+        hT = {}
+
+        def hidden(b, m):
+            if m == 0:
+                hT[b] = psum.tile([P, PACK, T], F32, name="hT", tag="bank_a")
             tok = slice(b * T, (b + 1) * T)
-            hT = psum.tile([P, PACK, T], F32, name="hT", tag="bank_a")
-            for m in range(PACK):
-                units = slice(m * P, (m + 1) * P)
-                for g in range(C_PASSES):
-                    nc.tensor.matmul_mx(
-                        out=hT[:, m, :],
-                        lhsT=w1_codes[:, g, units].bitcast(FP8X4),
-                        lhsT_scale=w1_scales[:, g, units],
-                        rhs=x_codes[:, g, tok].bitcast(FP8X4),
-                        rhs_scale=x_scales[:, g, tok],
-                        start=(g == 0),
-                        stop=(g == C_PASSES - 1),
-                    )
-            nc.scalar.activation(
-                out=h_grouped[b][:], in_=hT[:].rearrange("p m t -> p t m"), func=ACT.Tanh
-            )
+            units = slice(m * P, (m + 1) * P)
+            for g in range(C_PASSES):
+                nc.tensor.matmul_mx(
+                    out=hT[b][:, m, :],
+                    lhsT=w1_codes[:, g, units].bitcast(FP8X4),
+                    lhsT_scale=w1_scales[:, g, units],
+                    rhs=x_codes[:, g, tok].bitcast(FP8X4),
+                    rhs_scale=x_scales[:, g, tok],
+                    start=(g == 0),
+                    stop=(g == C_PASSES - 1),
+                )
+            if m == PACK - 1:
+                nc.scalar.activation(
+                    out=h_grouped[b][:], in_=hT[b][:].rearrange("p m t -> p t m"), func=ACT.Tanh
+                )
 
         def on_vector(grouped, planes):
             regroup(nc.vector.tensor_copy, grouped[:], planes[:])
@@ -261,13 +270,18 @@ def tile_full_tmix_params_pc_kernel(tc, x, x_w, w0, w1, w2, out):
         add_mix(last, 0)
         quantise_w1(last)
         quantise_x(last, slice(0, TOKENS // 2))
-        hidden(0)
-        hidden(1)
+        for m in range(PACK):
+            hidden(0, m)
+        for m in range(PACK):
+            hidden(1, m)
         add_mix(last, 1)
         quantise_w2(0)
         quantise_x(last, slice(TOKENS // 2, TOKENS))
         for c in range(1, C_BANKS):
             quantise_w2(c)
+        later_groups = [(b, m) for b in range(2, BATCH) for m in range(PACK)]
+        for m in range(2):
+            hidden(*later_groups.pop(0))
         quantise_h(0)
 
         z_all = []
@@ -294,8 +308,8 @@ def tile_full_tmix_params_pc_kernel(tc, x, x_w, w0, w1, w2, out):
                 nc.scalar.activation(
                     out=s[:, cols], in_=z[:, cols], func=ACT.Sigmoid, bias=half[:]
                 )
-                if c == 1 and b + 2 < BATCH:
-                    hidden(b + 2)
+                if later_groups:
+                    hidden(*later_groups.pop(0))
                 if c == 2 and b + 1 < BATCH:
                     quantise_h(b + 1)
             z_all.append(z)

@@ -22,7 +22,7 @@ DW = 512
 C_PASSES = C // K_PASS
 N_BANK = 512
 C_BANKS = C // N_BANK
-WIDE = 1024
+STORE = 1024
 TINY = 2.0 ** -60
 
 FLOPS = 2 * TOKENS * C * DW * 2
@@ -75,16 +75,17 @@ def tile_full_tmix_params_pc_kernel(tc, x, x_w, w0, w1, w2, out):
         x_sb = []
         w1_sb = []
 
-        def load_x(g):
-            x_g = keep.tile([P, BATCH, K_PASS], BF16, name="x_sb%d" % g)
-            loads = PACK if g == 0 else 1
-            width = K_PASS // loads
+        def load_x(first, passes, loads):
+            x_g = keep.tile([P, BATCH, passes * K_PASS], BF16, name="x_sb%d" % first)
+            c0 = first * K_PASS
+            width = passes * K_PASS // loads
             for i in range(loads):
                 nc.sync.dma_start(
                     out=x_g[:, :, i * width : (i + 1) * width],
-                    in_=x_by_token[:, :, g * K_PASS + i * width : g * K_PASS + (i + 1) * width],
+                    in_=x_by_token[:, :, c0 + i * width : c0 + (i + 1) * width],
                 )
-            x_sb.append(x_g)
+            for g in range(passes):
+                x_sb.append(x_g[:, :, g * K_PASS : (g + 1) * K_PASS])
 
         def load_w1(g):
             w1_g = keep.tile([P, PACK, DW], BF16, name="w1_sb%d" % g)
@@ -92,19 +93,25 @@ def tile_full_tmix_params_pc_kernel(tc, x, x_w, w0, w1, w2, out):
                 out=w1_g[:],
                 in_=w1[g * K_PASS : (g + 1) * K_PASS, :].rearrange("(j p) n -> p j n", p=P),
             )
-            w1_sb.append(w1_g)
+            w1_sb.append(w1_g[:])
 
-        load_x(0)
-        for g in range(1, C_PASSES):
-            load_x(g)
-            load_w1(g - 1)
-        load_w1(C_PASSES - 1)
+        load_x(0, 1, PACK)
+        load_x(1, 1, 1)
+        load_w1(0)
+        load_w1(1)
+        load_x(2, 2, 1)
+        load_w1(2)
+        load_w1(3)
         w2_by_k = w2.rearrange("(j p) n -> p j n", p=P)
         w2_sb = []
-        for c in range(C_BANKS):
-            w2_c = keep.tile([P, PACK, N_BANK], BF16, name="w2_sb%d" % c)
-            nc.sync.dma_start(out=w2_c[:], in_=w2_by_k[:, :, c * N_BANK : (c + 1) * N_BANK])
-            w2_sb.append(w2_c)
+        for i in range(2):
+            w2_half = keep.tile([P, PACK, 2 * N_BANK], BF16, name="w2_half%d" % i)
+            nc.sync.dma_start(
+                out=w2_half[:],
+                in_=w2_by_k[:, :, i * 2 * N_BANK : (i + 1) * 2 * N_BANK],
+            )
+            for c in range(2):
+                w2_sb.append(w2_half[:, :, c * N_BANK : (c + 1) * N_BANK])
         w0_bc = const.tile([P, C], BF16, name="w0_bc")
         nc.sync.dma_start(out=w0_bc[:], in_=w0.partition_broadcast(P))
 
@@ -242,19 +249,19 @@ def tile_full_tmix_params_pc_kernel(tc, x, x_w, w0, w1, w2, out):
                 )
 
         def on_vector(grouped, planes):
-            regroup(nc.vector.tensor_copy, grouped[:], planes[:])
+            regroup(nc.vector.tensor_copy, grouped[:], planes)
 
         def on_scalar(grouped, planes):
-            regroup(nc.scalar.copy, grouped[:], planes[:])
+            regroup(nc.scalar.copy, grouped[:], planes)
 
         first_pass()
-        on_vector(w1_grouped[0], w1_sb[0])
         regroup(
             nc.vector.tensor_copy, xw_grouped[0][:], xw_planes[:].rearrange("p j b t -> p j (b t)")
         )
+        on_vector(w1_grouped[0], w1_sb[0])
         diff_pass(1)
-        quantise_w1(0)
         quantise_x(0)
+        quantise_w1(0)
         last = C_PASSES - 1
         for g in range(1, last):
             on_scalar(w1_grouped[g], w1_sb[g])
@@ -316,13 +323,20 @@ def tile_full_tmix_params_pc_kernel(tc, x, x_w, w0, w1, w2, out):
             s_all.append(s)
 
         for b in range(BATCH):
-            width = WIDE if 0 < b < BATCH - 1 else N_BANK
+            pieces = [(c * N_BANK, (c + 1) * N_BANK) for c in range(C_BANKS)]
+            if b == BATCH - 1:
+                c0, c1 = pieces.pop()
+                pieces += [(c0, c0 + N_BANK // 2), (c0 + N_BANK // 2, c1)]
+            stored = 0
             s = s_all[b]
-            for piece in range(C // width):
-                cols = slice(piece * width, (piece + 1) * width)
-                nc.scalar.activation(out=s[:, cols], in_=s[:, cols], func=ACT.Ln, bias=tiny[:])
+            for c0, c1 in pieces:
+                nc.scalar.activation(
+                    out=s[:, c0:c1], in_=s[:, c0:c1], func=ACT.Ln, bias=tiny[:]
+                )
                 nc.vector.scalar_tensor_tensor(
-                    out=s[:, cols], in0=s[:, cols], scalar=-0.5, in1=z_all[b][:, cols],
+                    out=s[:, c0:c1], in0=s[:, c0:c1], scalar=-0.5, in1=z_all[b][:, c0:c1],
                     op0=ALU.add, op1=ALU.min,
                 )
-                nc.sync.dma_start(out=out[b, :, cols], in_=s[:, cols])
+                if b == BATCH - 1 or c1 - stored == STORE:
+                    nc.sync.dma_start(out=out[b, :, stored:c1], in_=s[:, stored:c1])
+                    stored = c1

from contextlib import ExitStack

from concourse import mybir
from concourse.masks import make_identity

BF16 = mybir.dt.bfloat16
F32 = mybir.dt.float32
U32 = mybir.dt.uint32
U8 = mybir.dt.uint8
FP8X4 = mybir.dt.float8_e4m3fn_x4
ALU = mybir.AluOpType
ACT = mybir.ActivationFunctionType

P = 128
PACK = 4
K_PASS = P * PACK
BATCH = 4
T = 128
TOKENS = BATCH * T
C = 2048
DW = 512
C_PASSES = C // K_PASS
N_BANK = 512
C_BANKS = C // N_BANK
STORE = 1024
TINY = 2.0 ** -60

FLOPS = 2 * TOKENS * C * DW * 2


def regroup(engine_copy, grouped, planes):
    engine_copy(
        out=grouped.rearrange("p (c i) j -> p c j i", i=4),
        in_=planes.rearrange("p j (c i) -> p c j i", i=4),
    )


def quantise(nc, grouped, codes, scales):
    nc.vector.quantize_mx(
        out=codes.bitcast(FP8X4),
        scales=scales,
        in_=grouped.rearrange("p w j -> p (w j)"),
    )


def tile_full_tmix_params_pc_kernel(tc, x, x_w, w0, w1, w2, out):
    nc = tc.nc
    with ExitStack() as stack:
        const = stack.enter_context(tc.tile_pool(name="const", bufs=1))
        keep = stack.enter_context(tc.tile_pool(name="keep", bufs=1))
        work = stack.enter_context(tc.tile_pool(name="work", bufs=2))
        psum = stack.enter_context(tc.psum_pool(name="psum", bufs=4))
        stack.enter_context(tc.manual_schedule())

        ident = const.tile([P, P], BF16, name="ident")
        make_identity(nc, ident[:])
        xw_rows = const.tile([P, P], BF16, name="xw_rows")
        nc.vector.memset(xw_rows[:], 0.0)
        half = const.tile([P, 1], F32, name="half")
        nc.vector.memset(half[:], 0.5)
        tiny = const.tile([P, 1], F32, name="tiny")
        nc.vector.memset(tiny[:], TINY)
        diff = const.tile([P, P], BF16, name="diff")
        nc.vector.tensor_scalar_mul(out=diff[:], in0=ident[:], scalar1=-1.0)
        nc.vector.tensor_tensor(
            out=diff[:, 1:P], in0=diff[:, 1:P], in1=ident[:, 0 : P - 1], op=ALU.add
        )
        warm = const.tile([P, 1], F32, name="warm")
        nc.scalar.activation(out=warm[:], in_=half[:], func=ACT.Sigmoid)

        nc.sync.dma_start(
            out=xw_rows[0 : C // P, :], in_=x_w.rearrange("(r c) -> r c", c=P)
        )
        x_by_token = x.rearrange("b t c -> t b c")
        x_sb = []
        w1_sb = []

        def load_x(first, passes, loads):
            x_g = keep.tile([P, BATCH, passes * K_PASS], BF16, name="x_sb%d" % first)
            c0 = first * K_PASS
            width = passes * K_PASS // loads
            for i in range(loads):
                nc.sync.dma_start(
                    out=x_g[:, :, i * width : (i + 1) * width],
                    in_=x_by_token[:, :, c0 + i * width : c0 + (i + 1) * width],
                )
            for g in range(passes):
                x_sb.append(x_g[:, :, g * K_PASS : (g + 1) * K_PASS])

        def load_w1(g):
            w1_g = keep.tile([P, PACK, DW], BF16, name="w1_sb%d" % g)
            nc.sync.dma_start(
                out=w1_g[:],
                in_=w1[g * K_PASS : (g + 1) * K_PASS, :].rearrange("(j p) n -> p j n", p=P),
            )
            w1_sb.append(w1_g[:])

        load_x(0, 1, PACK)
        load_x(1, 1, 1)
        load_w1(0)
        load_w1(1)
        load_x(2, 2, 1)
        load_w1(2)
        load_w1(3)
        w2_by_k = w2.rearrange("(j p) n -> p j n", p=P)
        w2_sb = []
        for i in range(2):
            w2_half = keep.tile([P, PACK, 2 * N_BANK], BF16, name="w2_half%d" % i)
            nc.sync.dma_start(
                out=w2_half[:],
                in_=w2_by_k[:, :, i * 2 * N_BANK : (i + 1) * 2 * N_BANK],
            )
            for c in range(2):
                w2_sb.append(w2_half[:, :, c * N_BANK : (c + 1) * N_BANK])
        w0_bc = const.tile([P, C], BF16, name="w0_bc")
        nc.sync.dma_start(out=w0_bc[:], in_=w0.partition_broadcast(P))

        prev = []
        for j in range(PACK):
            prev_j = keep.tile([P, BATCH, T + 1], F32, name="prev%d" % j)
            nc.vector.memset(prev_j[:, :, 0:1], 0.0)
            prev.append(prev_j)

        mix_ps = psum.tile([P, P], BF16, name="mix_ps", tag="bank_a")
        nc.tensor.transpose(mix_ps[:], xw_rows[:], ident[:])
        mix = const.tile([P, C // P], F32, name="mix")
        nc.vector.tensor_copy(out=mix[:], in_=mix_ps[:, 0 : C // P])
        one_minus_mix = const.tile([P, C // P], F32, name="one_minus_mix")
        nc.vector.tensor_scalar(
            out=one_minus_mix[:], in0=mix_ps[:, 0 : C // P],
            scalar1=-1.0, scalar2=1.0, op0=ALU.mult, op1=ALU.add,
        )

        x_codes = keep.tile([P, C_PASSES, TOKENS], U32, name="x_codes", align_bytes=64)
        x_scales = keep.tile([P, C_PASSES, TOKENS], U8, name="x_scales", align_bytes=64)
        w1_codes = keep.tile([P, C_PASSES, DW], U32, name="w1_codes", align_bytes=64)
        w1_scales = keep.tile([P, C_PASSES, DW], U8, name="w1_scales", align_bytes=64)
        w2_codes = keep.tile([P, C_BANKS, N_BANK], U32, name="w2_codes", align_bytes=64)
        w2_scales = keep.tile([P, C_BANKS, N_BANK], U8, name="w2_scales", align_bytes=64)
        h_codes = keep.tile([P, BATCH, T], U32, name="h_codes", align_bytes=64)
        h_scales = keep.tile([P, BATCH, T], U8, name="h_scales", align_bytes=64)

        xw_grouped = []
        w1_grouped = []
        for g in range(C_PASSES):
            xw_grouped.append(
                work.tile([P, TOKENS, PACK], BF16, name="xw_grouped%d" % g, bufs=1, align_bytes=64)
            )
            w1_grouped.append(
                work.tile([P, DW, PACK], BF16, name="w1_grouped%d" % g, bufs=1, align_bytes=64)
            )
        h_grouped = []
        for b in range(BATCH):
            h_grouped.append(
                work.tile([P, T, PACK], BF16, name="h_grouped%d" % b, bufs=1, align_bytes=64)
            )
        w2_grouped = []
        for c in range(C_BANKS):
            w2_grouped.append(
                work.tile([P, N_BANK, PACK], BF16, name="w2_grouped%d" % c, bufs=1, align_bytes=64)
            )
        xw_planes = work.tile([P, PACK, BATCH, T], BF16, name="xw_planes", bufs=1)

        def first_pass():
            for j in range(PACK):
                xT = psum.tile([P, BATCH, T], BF16, name="xT", tag="bank_b")
                for b in range(BATCH):
                    nc.tensor.transpose(xT[:, b, :], x_sb[0][:, b, j * P : (j + 1) * P], ident[:])
                nc.scalar.activation(
                    out=prev[j][:, :, 1 : T + 1], in_=xT[:], func=ACT.Copy,
                    scale=mix[:, j : j + 1],
                )
                nc.vector.scalar_tensor_tensor(
                    out=xw_planes[:, j, :, :], in0=xT[:],
                    scalar=one_minus_mix[:, j : j + 1],
                    in1=prev[j][:, :, 0:T], op0=ALU.mult, op1=ALU.add,
                )

        halves = {}
        dms = {}

        def diff_pass(g):
            halves[g] = []
            for h in range(2):
                halves[g].append(
                    psum.tile([P, PACK, TOKENS // 2], BF16, name="xT_half%d" % h, tag="bank_a")
                )
            dms[g] = work.tile([P, PACK, TOKENS], F32, name="dm")
            for j in range(PACK):
                chunk = g * PACK + j
                d_ps = psum.tile([P, BATCH, T], F32, name="d_ps", tag="bank_b")
                for b in range(BATCH):
                    block = x_sb[g][:, b, j * P : (j + 1) * P]
                    nc.tensor.matmul(d_ps[:, b, :], lhsT=block, rhs=diff[:], start=True, stop=True)
                nc.scalar.activation(
                    out=dms[g][:, j, :], in_=d_ps[:].rearrange("p b t -> p (b t)"), func=ACT.Copy,
                    scale=mix[:, chunk : chunk + 1],
                )
            for h in range(2):
                for j in range(PACK):
                    for b in range(2):
                        nc.tensor.transpose(
                            halves[g][h][:, j, b * T : (b + 1) * T],
                            x_sb[g][:, 2 * h + b, j * P : (j + 1) * P],
                            ident[:],
                        )

        def add_mix(g, h):
            toks = slice(h * TOKENS // 2, (h + 1) * TOKENS // 2)
            nc.vector.tensor_tensor(
                out=xw_grouped[g][:, toks, :].rearrange("p (c i) j -> p c j i", i=2),
                in0=halves[g][h][:].rearrange("p j (c i) -> p c j i", i=2),
                in1=dms[g][:, :, toks].rearrange("p j (c i) -> p c j i", i=2),
                op=ALU.add,
            )

        def quantise_x(g, toks=slice(0, TOKENS)):
            quantise(nc, xw_grouped[g][:, toks, :], x_codes[:, g, toks], x_scales[:, g, toks])

        def quantise_w1(g):
            quantise(nc, w1_grouped[g][:], w1_codes[:, g, :], w1_scales[:, g, :])

        def quantise_w2(c):
            quantise(nc, w2_grouped[c][:], w2_codes[:, c, :], w2_scales[:, c, :])

        def quantise_h(b):
            quantise(nc, h_grouped[b][:], h_codes[:, b, :], h_scales[:, b, :])

        hT = {}

        def hidden(b, m):
            if m == 0:
                hT[b] = psum.tile([P, PACK, T], F32, name="hT", tag="bank_a")
            tok = slice(b * T, (b + 1) * T)
            units = slice(m * P, (m + 1) * P)
            for g in range(C_PASSES):
                nc.tensor.matmul_mx(
                    out=hT[b][:, m, :],
                    lhsT=w1_codes[:, g, units].bitcast(FP8X4),
                    lhsT_scale=w1_scales[:, g, units],
                    rhs=x_codes[:, g, tok].bitcast(FP8X4),
                    rhs_scale=x_scales[:, g, tok],
                    start=(g == 0),
                    stop=(g == C_PASSES - 1),
                )
            if m == PACK - 1:
                nc.scalar.activation(
                    out=h_grouped[b][:], in_=hT[b][:].rearrange("p m t -> p t m"), func=ACT.Tanh
                )

        def on_vector(grouped, planes):
            regroup(nc.vector.tensor_copy, grouped[:], planes)

        def on_scalar(grouped, planes):
            regroup(nc.scalar.copy, grouped[:], planes)

        first_pass()
        regroup(
            nc.vector.tensor_copy, xw_grouped[0][:], xw_planes[:].rearrange("p j b t -> p j (b t)")
        )
        on_vector(w1_grouped[0], w1_sb[0])
        diff_pass(1)
        quantise_x(0)
        quantise_w1(0)
        last = C_PASSES - 1
        for g in range(1, last):
            on_scalar(w1_grouped[g], w1_sb[g])
            add_mix(g, 0)
            add_mix(g, 1)
            diff_pass(g + 1)
            quantise_w1(g)
            quantise_x(g)
        on_vector(w2_grouped[0], w2_sb[0])
        on_vector(w1_grouped[last], w1_sb[last])
        for c in range(1, C_BANKS):
            on_scalar(w2_grouped[c], w2_sb[c])
        add_mix(last, 0)
        quantise_w1(last)
        quantise_x(last, slice(0, TOKENS // 2))
        for m in range(PACK):
            hidden(0, m)
        for m in range(PACK):
            hidden(1, m)
        add_mix(last, 1)
        quantise_w2(0)
        quantise_x(last, slice(TOKENS // 2, TOKENS))
        for c in range(1, C_BANKS):
            quantise_w2(c)
        later_groups = [(b, m) for b in range(2, BATCH) for m in range(PACK)]
        for m in range(2):
            hidden(*later_groups.pop(0))
        quantise_h(0)

        z_all = []
        s_all = []
        for b in range(BATCH):
            z = keep.tile([P, C], F32, name="z%d" % b)
            s = keep.tile([P, C], F32, name="s%d" % b)
            for c in range(C_BANKS):
                cols = slice(c * N_BANK, (c + 1) * N_BANK)
                z_ps = psum.tile([P, N_BANK], F32, name="z_ps", tag="bank_a" if c % 2 else "bank_b")
                nc.tensor.matmul_mx(
                    out=z_ps[:],
                    lhsT=h_codes[:, b, :].bitcast(FP8X4),
                    lhsT_scale=h_scales[:, b, :],
                    rhs=w2_codes[:, c, :].bitcast(FP8X4),
                    rhs_scale=w2_scales[:, c, :],
                    start=True,
                    stop=True,
                )
                nc.vector.scalar_tensor_tensor(
                    out=z[:, cols], in0=z_ps[:], scalar=-0.5, in1=w0_bc[:, cols],
                    op0=ALU.add, op1=ALU.add,
                )
                nc.scalar.activation(
                    out=s[:, cols], in_=z[:, cols], func=ACT.Sigmoid, bias=half[:]
                )
                if later_groups:
                    hidden(*later_groups.pop(0))
                if c == 2 and b + 1 < BATCH:
                    quantise_h(b + 1)
            z_all.append(z)
            s_all.append(s)

        for b in range(BATCH):
            pieces = [(c * N_BANK, (c + 1) * N_BANK) for c in range(C_BANKS)]
            if b == BATCH - 1:
                c0, c1 = pieces.pop()
                pieces += [(c0, c0 + N_BANK // 2), (c0 + N_BANK // 2, c1)]
            stored = 0
            s = s_all[b]
            for c0, c1 in pieces:
                nc.scalar.activation(
                    out=s[:, c0:c1], in_=s[:, c0:c1], func=ACT.Ln, bias=tiny[:]
                )
                nc.vector.scalar_tensor_tensor(
                    out=s[:, c0:c1], in0=s[:, c0:c1], scalar=-0.5, in1=z_all[b][:, c0:c1],
                    op0=ALU.add, op1=ALU.min,
                )
                if b == BATCH - 1 or c1 - stored == STORE:
                    nc.sync.dma_start(out=out[b, :, stored:c1], in_=s[:, stored:c1])
                    stored = c1
